import numpy as np
import ml_dtypes


def mxq(x, axis, fmt="e4m3"):
    dtype, down = {"e4m3": (ml_dtypes.float8_e4m3fn, 7), "e5m2": (ml_dtypes.float8_e5m2, 14)}[fmt]
    v = np.moveaxis(np.asarray(x, np.float32).astype(ml_dtypes.bfloat16).astype(np.float64), axis, -1)
    blocks = v.reshape(v.shape[:-1] + (-1, 32))
    amax = np.abs(blocks).max(-1, keepdims=True)
    byte = np.maximum(np.where(amax > 0, np.frexp(amax)[1] - 1 + 127, 0) - down, 1)
    scale = np.exp2(byte - 127.0)
    codes = (blocks / scale).astype(np.float32).astype(dtype).astype(np.float64)
    return np.moveaxis((codes * scale).reshape(v.shape), -1, axis)


WIDE = False


def mx_kscale(k):
    if not WIDE:
        return np.ones(k)
    levels = np.array([10, -10, 5, -5, 0])
    a = np.random.permutation(np.resize(levels, k // 512 * 4)).reshape(k // 512, 4)
    idx = np.arange(k)
    return np.exp2(a[idx // 512, idx % 128 // 32])


BF16 = ml_dtypes.bfloat16


def bf(x):
    return np.asarray(x, np.float32).astype(BF16)


def f64(x):
    return np.asarray(x).astype(np.float64)


N, S, D, H, O = 4, 256, 1024, 1024, 1024


def elu(v):
    return np.where(v > 0.0, v, np.exp(np.minimum(v, 0.0)) - 1.0)


def setup_inputs():
    s = mx_kscale(D)
    return {"x": bf(np.random.standard_normal((N, S, D)) * s),
            "Wk": bf(np.random.standard_normal((D, H)) / np.sqrt(D) / s[:, None]),
            "bk": bf(np.random.standard_normal(H) * 0.1),
            "Wv": bf(np.random.standard_normal((D, H)) / np.sqrt(D) / s[:, None]),
            "bv": bf(np.random.standard_normal(H) * 0.1)}


def reference(x, Wk, bk, Wv, bv):
    xq = mxq(f64(x), 2, "e4m3")
    keyp = (xq @ mxq(f64(Wk), 0, "e4m3")) + f64(bk)
    value = (xq @ mxq(f64(Wv), 0, "e4m3")) + f64(bv)
    K = elu(keyp) + 1.0
    KV = np.sum(K * value, axis=1)
    Ksum = np.sum(K, axis=1)
    return KV, Ksum

@@ -1,0 +1,305 @@
+from contextlib import ExitStack
+from itertools import product
+
+import concourse.mybir as mybir
+from concourse.masks import make_identity
+
+F32 = mybir.dt.float32
+BF16 = mybir.dt.bfloat16
+U32 = mybir.dt.uint32
+U8 = mybir.dt.uint8
+FP8X4 = mybir.dt.float8_e4m3fn_x4
+ALU = mybir.AluOpType
+ACT = mybir.ActivationFunctionType
+
+BATCHES, SEQ, D, H = 4, 256, 1024, 1024
+TOKENS = BATCHES * SEQ
+
+P = 128
+PACK = 4
+K_PASS = P * PACK
+PASSES = D // K_PASS
+WORDS = PACK // 2
+
+N_MOVE = 512
+HALVES = TOKENS // N_MOVE
+TOKEN_TILES = TOKENS // P
+TILES_PER_HALF = N_MOVE // P
+BATCHES_PER_HALF = N_MOVE // SEQ
+
+H_TILES = H // P
+CHUNK = 256
+CHUNKS = H // CHUNK
+TILES_PER_CHUNK = CHUNK // P
+WEIGHTS = 2
+PIECES = WEIGHTS * PASSES * CHUNKS
+KEY, VALUE = 0, 1
+
+UNITS = H_TILES * HALVES
+UNITS_PER_CHUNK = TILES_PER_CHUNK * HALVES
+
+RUN = 8
+
+KEYS_AHEAD = 2
+EXP_AHEAD = 1
+
+GPSIMD_PIECES = 3
+
+FLOPS = 2 * WEIGHTS * TOKENS * D * H
+
+
+def tile_linearattention_pa_kernel(tc, x, Wk, bk, Wv, bv, out_0, out_1):
+    nc = tc.nc
+    x_rows = x.rearrange("n s d -> (n s) d")
+    weights = (Wk, Wv)
+
+    with ExitStack() as ctx:
+        ctx.enter_context(tc.manual_schedule())
+        consts = ctx.enter_context(tc.tile_pool(name="consts", bufs=1))
+        x_pool = ctx.enter_context(tc.tile_pool(name="x_pool", bufs=1))
+        w_pool = ctx.enter_context(tc.tile_pool(name="w_pool", bufs=PIECES))
+        group_pool = ctx.enter_context(tc.tile_pool(name="group_pool", bufs=1))
+        work = ctx.enter_context(tc.tile_pool(name="work", bufs=3))
+        psum = ctx.enter_context(tc.psum_pool(name="psum", bufs=4))
+        bank_tags = ("key_acc", "value_acc")
+
+        bias_rows = consts.tile([P, P], BF16)
+        nc.vector.memset(bias_rows[:], 0.0)
+        nc.scalar.dma_start(out=bias_rows[0:H_TILES, :], in_=bk.rearrange("(t p) -> t p", p=P))
+        nc.scalar.dma_start(out=bias_rows[H_TILES : 2 * H_TILES, :], in_=bv.rearrange("(t p) -> t p", p=P))
+
+        x_raw = {}
+        w_raw = {}
+
+        def load_x_half(half):
+            for a in range(half * TILES_PER_HALF, (half + 1) * TILES_PER_HALF):
+                raw = x_pool.tile([P, D], BF16, tag="x_raw", bufs=TOKEN_TILES)
+                nc.sync.dma_start(out=raw[:], in_=x_rows[a * P : (a + 1) * P, :])
+                x_raw[a] = raw
+
+        def load_weight_chunk(c, w):
+            for g in range(PASSES):
+                raw = w_pool.tile([P, PACK, CHUNK], BF16, tag="w_raw")
+                nc.sync.dma_start(
+                    out=raw[:],
+                    in_=weights[w][g * K_PASS : (g + 1) * K_PASS, c * CHUNK : (c + 1) * CHUNK].rearrange(
+                        "(p j) c -> p j c", j=PACK
+                    ),
+                )
+                w_raw[(c, w, g)] = raw
+
+        load_x_half(0)
+        load_weight_chunk(0, KEY)
+        load_x_half(1)
+        load_weight_chunk(0, VALUE)
+        for c, w in product(range(1, CHUNKS), range(WEIGHTS)):
+            load_weight_chunk(c, w)
+
+        ident = consts.tile([P, P], F32)
+        make_identity(nc, ident[:])
+
+        warm = consts.tile([P, 1], F32)
+        nc.vector.memset(warm[:], 0.0)
+        nc.scalar.activation(out=warm[:], in_=warm[:], func=ACT.Exp)
+
+        sums = consts.tile([P, P], F32)
+        nc.vector.memset(sums[:], 0.0)
+
+        x_grouped = {}
+        x_quant = {}
+
+        def transpose_x_half(half):
+            grouped = x_pool.tile([P, PASSES * N_MOVE * PACK], BF16, align_bytes=64, tag="x_grouped", bufs=HALVES)
+            grouped_words = grouped[:].bitcast(F32).rearrange("p (g t u) -> p g t u", g=PASSES, u=WORDS)
+            for a in range(TILES_PER_HALF):
+                words = (
+                    x_raw[half * TILES_PER_HALF + a][:]
+                    .bitcast(F32)
+                    .rearrange("p (g q u) -> p g u q", g=PASSES, u=WORDS)
+                )
+                transposed = psum.tile([P, PASSES, WORDS, P], F32, tag=bank_tags[a % 2])
+                for g, u in product(range(PASSES), range(WORDS)):
+                    nc.tensor.transpose(out=transposed[:, g, u, :], in_=words[:, g, u, :], identity=ident[:])
+                nc.scalar.copy(
+                    out=grouped_words[:, :, a * P : (a + 1) * P, :],
+                    in_=transposed[:].rearrange("p g u t -> p g t u"),
+                )
+            x_grouped[half] = grouped
+
+        def quantise_x_half(half):
+            for g in range(PASSES):
+                codes = x_pool.tile([P, N_MOVE], U32, align_bytes=64, tag="x_codes", bufs=HALVES * PASSES)
+                scales = x_pool.tile([P, N_MOVE], U8, align_bytes=64, tag="x_scales", bufs=HALVES * PASSES)
+                nc.vector.quantize_mx(
+                    out=codes[:].bitcast(FP8X4),
+                    scales=scales[:],
+                    in_=x_grouped[half][:, g * N_MOVE * PACK : (g + 1) * N_MOVE * PACK],
+                )
+                x_quant[(g, half)] = (codes, scales)
+
+        w_grouped = {}
+        w_quant = {}
+
+        def regroup_weight_piece(c, w, g, engine):
+            if c not in w_grouped:
+                w_grouped[c] = group_pool.tile(
+                    [P, WEIGHTS, PASSES, CHUNK, PACK], BF16, align_bytes=64, name="w_grouped", tag="w_grouped"
+                )
+            grouped = w_grouped[c][:, w, g]
+            raw = w_raw[(c, w, g)][:]
+            if engine == "gpsimd":
+                nc.gpsimd.tensor_scalar(
+                    out=grouped,
+                    in0=raw.rearrange("p j c -> p c j"),
+                    scalar1=1.0,
+                    scalar2=0.0,
+                    op0=ALU.mult,
+                    op1=ALU.add,
+                )
+            else:
+                copy = nc.vector.tensor_copy if engine == "vector" else nc.scalar.copy
+                copy(
+                    out=grouped.rearrange("p (c i) j -> p c j i", i=RUN),
+                    in_=raw.rearrange("p j (c i) -> p c j i", i=RUN),
+                )
+
+        def quantise_weight_chunk(c, w):
+            codes = w_pool.tile([P, PASSES, CHUNK], U32, align_bytes=64, tag="w_codes", bufs=WEIGHTS * CHUNKS)
+            scales = w_pool.tile([P, PASSES, CHUNK], U8, align_bytes=64, tag="w_scales", bufs=WEIGHTS * CHUNKS)
+            nc.vector.quantize_mx(
+                out=codes[:].rearrange("p g c -> p (g c)").bitcast(FP8X4),
+                scales=scales[:].rearrange("p g c -> p (g c)"),
+                in_=w_grouped[c][:, w].rearrange("p g c j -> p (g c j)"),
+            )
+            w_quant[(c, w)] = (codes, scales)
+
+        def unit_place(i):
+            c, rest = divmod(i, UNITS_PER_CHUNK)
+            half, local = divmod(rest, TILES_PER_CHUNK)
+            return c, local, half
+
+        def multiply(w, i, acc):
+            c, local, half = unit_place(i)
+            cols = slice(local * P, (local + 1) * P)
+            w_codes, w_scales = w_quant[(c, w)]
+            for g in range(PASSES):
+                x_codes, x_scales = x_quant[(g, half)]
+                nc.tensor.matmul_mx(
+                    out=acc[:],
+                    lhsT=w_codes[:, g, cols].bitcast(FP8X4),
+                    lhsT_scale=w_scales[:, g, cols],
+                    rhs=x_codes[:].bitcast(FP8X4),
+                    rhs_scale=x_scales[:],
+                    start=(g == 0),
+                    stop=(g == PASSES - 1),
+                )
+
+        key_acc = {}
+        value_acc = {}
+        relu_minus_v = {}
+        exp_min_v_0 = {}
+
+        def stage_keys(i):
+            c, local, half = unit_place(i)
+            t = c * TILES_PER_CHUNK + local
+            key_acc[i] = psum.tile([P, N_MOVE], F32, tag="key_acc", name="key_acc")
+            multiply(KEY, i, key_acc[i])
+            relu_minus_v[i] = work.tile([P, N_MOVE], F32, tag="relu_minus_v", name="relu_minus_v")
+            nc.scalar.activation(
+                out=relu_minus_v[i][:], in_=key_acc[i][:], func=ACT.Relu, scale=-1.0, bias=minus_bk[:, t : t + 1]
+            )
+
+        def stage_exp(i):
+            exp_min_v_0[i] = work.tile([P, N_MOVE], F32, tag="exp_min_v_0", name="exp_min_v_0")
+            nc.scalar.activation(out=exp_min_v_0[i][:], in_=relu_minus_v[i][:], func=ACT.Exp, scale=-1.0)
+
+        def stage_values(i):
+            value_acc[i] = psum.tile([P, N_MOVE], F32, tag="value_acc", name="value_acc")
+            multiply(VALUE, i, value_acc[i])
+
+        def stage_sums(i):
+            c, local, half = unit_place(i)
+            t = c * TILES_PER_CHUNK + local
+            k_feat = work.tile([P, N_MOVE], F32, tag="k_feat")
+            k_value = work.tile([P, N_MOVE], F32, tag="k_value")
+            for b in range(BATCHES_PER_HALF):
+                toks = slice(b * SEQ, (b + 1) * SEQ)
+                ksum_col = BATCHES * H_TILES + (half * BATCHES_PER_HALF + b) * H_TILES + t
+                nc.vector.scalar_tensor_tensor(
+                    out=k_feat[:, toks],
+                    in0=key_acc[i][:, toks],
+                    scalar=bk_plus_1[:, t : t + 1],
+                    in1=exp_min_v_0[i][:, toks],
+                    op0=ALU.add,
+                    op1=ALU.max,
+                    accum_out=sums[:, ksum_col : ksum_col + 1],
+                )
+            for b in range(BATCHES_PER_HALF):
+                toks = slice(b * SEQ, (b + 1) * SEQ)
+                kv_col = (half * BATCHES_PER_HALF + b) * H_TILES + t
+                nc.vector.scalar_tensor_tensor(
+                    out=k_value[:, toks],
+                    in0=value_acc[i][:, toks],
+                    scalar=bv_cols[:, t : t + 1],
+                    in1=k_feat[:, toks],
+                    op0=ALU.add,
+                    op1=ALU.mult,
+                    accum_out=sums[:, kv_col : kv_col + 1],
+                )
+
+        transpose_x_half(0)
+
+        bias_rows_f32 = consts.tile([P, P], F32)
+        nc.vector.tensor_copy(out=bias_rows_f32[:], in_=bias_rows[:])
+        bias_ps = psum.tile([P, P], F32, tag="key_acc")
+        nc.tensor.transpose(out=bias_ps[:], in_=bias_rows_f32[:], identity=ident[:])
+        bv_cols = consts.tile([P, H_TILES], F32)
+        nc.vector.tensor_copy(out=bv_cols[:], in_=bias_ps[:, H_TILES : 2 * H_TILES])
+        bk_plus_1 = consts.tile([P, H_TILES], F32)
+        nc.vector.tensor_scalar_add(out=bk_plus_1[:], in0=bias_ps[:, 0:H_TILES], scalar1=1.0)
+        minus_bk = consts.tile([P, H_TILES], F32)
+        nc.vector.tensor_scalar_mul(out=minus_bk[:], in0=bias_ps[:, 0:H_TILES], scalar1=-1.0)
+
+        for g in range(PASSES):
+            regroup_weight_piece(0, KEY, g, "vector")
+        quantise_x_half(0)
+        quantise_weight_chunk(0, KEY)
+        transpose_x_half(1)
+        for g in range(PASSES):
+            regroup_weight_piece(0, VALUE, g, "vector")
+        quantise_weight_chunk(0, VALUE)
+        quantise_x_half(1)
+
+        pieces = list(product(range(WEIGHTS), range(PASSES)))
+        for w, g in pieces[:GPSIMD_PIECES]:
+            regroup_weight_piece(1, w, g, "gpsimd")
+
+        for i in range(-KEYS_AHEAD, UNITS):
+            if 0 <= i + EXP_AHEAD < UNITS:
+                stage_exp(i + EXP_AHEAD)
+            if i + KEYS_AHEAD < UNITS:
+                stage_keys(i + KEYS_AHEAD)
+            if 0 <= i + EXP_AHEAD < UNITS:
+                stage_values(i + EXP_AHEAD)
+            if i < 0:
+                continue
+            c, place_in_chunk = divmod(i, UNITS_PER_CHUNK)
+            more_chunks = c + 1 < CHUNKS
+            if more_chunks and place_in_chunk < len(pieces) - GPSIMD_PIECES:
+                regroup_weight_piece(c + 1, *pieces[GPSIMD_PIECES + place_in_chunk], "scalar")
+            stage_sums(i)
+            if more_chunks and place_in_chunk == UNITS_PER_CHUNK - KEYS_AHEAD - 1:
+                quantise_weight_chunk(c + 1, KEY)
+            if more_chunks and place_in_chunk == UNITS_PER_CHUNK - EXP_AHEAD - 1:
+                quantise_weight_chunk(c + 1, VALUE)
+                if c + 2 < CHUNKS:
+                    for w, g in pieces[:GPSIMD_PIECES]:
+                        regroup_weight_piece(c + 2, w, g, "gpsimd")
+
+        sums_ps = psum.tile([P, P], F32, tag="key_acc")
+        nc.tensor.transpose(out=sums_ps[:], in_=sums[:], identity=ident[:])
+        result = consts.tile([P, P], F32)
+        nc.vector.tensor_copy(out=result[:], in_=sums_ps[:])
+        rows = BATCHES * H_TILES
+        nc.sync.dma_start(out=out_0.rearrange("n (t p) -> (n t) p", p=P), in_=result[0:rows, :])
+        nc.sync.dma_start(out=out_1.rearrange("n (t p) -> (n t) p", p=P), in_=result[rows : 2 * rows, :])

@@ -24,7 +24,7 @@ WORDS = PACK // 2
 N_MOVE = 512
 HALVES = TOKENS // N_MOVE
 TOKEN_TILES = TOKENS // P
-TILES_PER_HALF = N_MOVE // P
+TILES_PER_BATCH = SEQ // P
 BATCHES_PER_HALF = N_MOVE // SEQ
 
 H_TILES = H // P
@@ -44,6 +44,8 @@ KEYS_AHEAD = 2
 EXP_AHEAD = 1
 
 GPSIMD_PIECES = 3
+
+SCALAR_PIECES_OF_CHUNK_1 = ((KEY, 1), (VALUE, 1))
 
 FLOPS = 2 * WEIGHTS * TOKENS * D * H
 
@@ -71,11 +73,12 @@ def tile_linearattention_pa_kernel(tc, x, Wk, bk, Wv, bv, out_0, out_1):
         x_raw = {}
         w_raw = {}
 
-        def load_x_half(half):
-            for a in range(half * TILES_PER_HALF, (half + 1) * TILES_PER_HALF):
+        def load_x_batches(*batches):
+            for b, a in product(batches, range(TILES_PER_BATCH)):
                 raw = x_pool.tile([P, D], BF16, tag="x_raw", bufs=TOKEN_TILES)
-                nc.sync.dma_start(out=raw[:], in_=x_rows[a * P : (a + 1) * P, :])
-                x_raw[a] = raw
+                first = b * SEQ + a * P
+                nc.sync.dma_start(out=raw[:], in_=x_rows[first : first + P, :])
+                x_raw[(b, a)] = raw
 
         def load_weight_chunk(c, w):
             for g in range(PASSES):
@@ -88,9 +91,9 @@ def tile_linearattention_pa_kernel(tc, x, Wk, bk, Wv, bv, out_0, out_1):
                 )
                 w_raw[(c, w, g)] = raw
 
-        load_x_half(0)
+        load_x_batches(0, 1)
         load_weight_chunk(0, KEY)
-        load_x_half(1)
+        load_x_batches(2, 3)
         load_weight_chunk(0, VALUE)
         for c, w in product(range(1, CHUNKS), range(WEIGHTS)):
             load_weight_chunk(c, w)
@@ -108,15 +111,11 @@ def tile_linearattention_pa_kernel(tc, x, Wk, bk, Wv, bv, out_0, out_1):
         x_grouped = {}
         x_quant = {}
 
-        def transpose_x_half(half):
-            grouped = x_pool.tile([P, PASSES * N_MOVE * PACK], BF16, align_bytes=64, tag="x_grouped", bufs=HALVES)
+        def transpose_x_batch(b):
+            grouped = x_pool.tile([P, PASSES * SEQ * PACK], BF16, align_bytes=64, tag="x_grouped", bufs=BATCHES)
             grouped_words = grouped[:].bitcast(F32).rearrange("p (g t u) -> p g t u", g=PASSES, u=WORDS)
-            for a in range(TILES_PER_HALF):
-                words = (
-                    x_raw[half * TILES_PER_HALF + a][:]
-                    .bitcast(F32)
-                    .rearrange("p (g q u) -> p g u q", g=PASSES, u=WORDS)
-                )
+            for a in range(TILES_PER_BATCH):
+                words = x_raw[(b, a)][:].bitcast(F32).rearrange("p (g q u) -> p g u q", g=PASSES, u=WORDS)
                 transposed = psum.tile([P, PASSES, WORDS, P], F32, tag=bank_tags[a % 2])
                 for g, u in product(range(PASSES), range(WORDS)):
                     nc.tensor.transpose(out=transposed[:, g, u, :], in_=words[:, g, u, :], identity=ident[:])
@@ -124,18 +123,22 @@ def tile_linearattention_pa_kernel(tc, x, Wk, bk, Wv, bv, out_0, out_1):
                     out=grouped_words[:, :, a * P : (a + 1) * P, :],
                     in_=transposed[:].rearrange("p g u t -> p g t u"),
                 )
-            x_grouped[half] = grouped
+            x_grouped[b] = grouped
 
-        def quantise_x_half(half):
+        def quantise_x_batch(b):
+            half, place = divmod(b, BATCHES_PER_HALF)
+            toks = slice(place * SEQ, (place + 1) * SEQ)
             for g in range(PASSES):
-                codes = x_pool.tile([P, N_MOVE], U32, align_bytes=64, tag="x_codes", bufs=HALVES * PASSES)
-                scales = x_pool.tile([P, N_MOVE], U8, align_bytes=64, tag="x_scales", bufs=HALVES * PASSES)
+                if place == 0:
+                    codes = x_pool.tile([P, N_MOVE], U32, align_bytes=64, tag="x_codes", bufs=HALVES * PASSES)
+                    scales = x_pool.tile([P, N_MOVE], U8, align_bytes=64, tag="x_scales", bufs=HALVES * PASSES)
+                    x_quant[(g, half)] = (codes, scales)
+                codes, scales = x_quant[(g, half)]
                 nc.vector.quantize_mx(
-                    out=codes[:].bitcast(FP8X4),
-                    scales=scales[:],
-                    in_=x_grouped[half][:, g * N_MOVE * PACK : (g + 1) * N_MOVE * PACK],
+                    out=codes[:, toks].bitcast(FP8X4),
+                    scales=scales[:, toks],
+                    in_=x_grouped[b][:, g * SEQ * PACK : (g + 1) * SEQ * PACK],
                 )
-                x_quant[(g, half)] = (codes, scales)
 
         w_grouped = {}
         w_quant = {}
@@ -247,36 +250,42 @@ def tile_linearattention_pa_kernel(tc, x, Wk, bk, Wv, bv, out_0, out_1):
                     accum_out=sums[:, kv_col : kv_col + 1],
                 )
 
-        transpose_x_half(0)
-
+        transpose_x_batch(0)
+        quantise_x_batch(0)
+        transpose_x_batch(1)
+        regroup_weight_piece(0, KEY, 0, "vector")
         bias_rows_f32 = consts.tile([P, P], F32)
         nc.vector.tensor_copy(out=bias_rows_f32[:], in_=bias_rows[:])
         bias_ps = psum.tile([P, P], F32, tag="key_acc")
         nc.tensor.transpose(out=bias_ps[:], in_=bias_rows_f32[:], identity=ident[:])
+        quantise_x_batch(1)
+        regroup_weight_piece(0, KEY, 1, "vector")
+        quantise_weight_chunk(0, KEY)
         bv_cols = consts.tile([P, H_TILES], F32)
         nc.vector.tensor_copy(out=bv_cols[:], in_=bias_ps[:, H_TILES : 2 * H_TILES])
         bk_plus_1 = consts.tile([P, H_TILES], F32)
         nc.vector.tensor_scalar_add(out=bk_plus_1[:], in0=bias_ps[:, 0:H_TILES], scalar1=1.0)
         minus_bk = consts.tile([P, H_TILES], F32)
         nc.vector.tensor_scalar_mul(out=minus_bk[:], in0=bias_ps[:, 0:H_TILES], scalar1=-1.0)
-
-        for g in range(PASSES):
-            regroup_weight_piece(0, KEY, g, "vector")
-        quantise_x_half(0)
-        quantise_weight_chunk(0, KEY)
-        transpose_x_half(1)
-        for g in range(PASSES):
-            regroup_weight_piece(0, VALUE, g, "vector")
+        transpose_x_batch(2)
+        quantise_x_batch(2)
+        transpose_x_batch(3)
+        regroup_weight_piece(0, VALUE, 0, "vector")
+        quantise_x_batch(3)
+        regroup_weight_piece(0, VALUE, 1, "vector")
         quantise_weight_chunk(0, VALUE)
-        quantise_x_half(1)
 
         pieces = list(product(range(WEIGHTS), range(PASSES)))
-        for w, g in pieces[:GPSIMD_PIECES]:
-            regroup_weight_piece(1, w, g, "gpsimd")
+        for w, g in pieces:
+            if (w, g) not in SCALAR_PIECES_OF_CHUNK_1:
+                regroup_weight_piece(1, w, g, "gpsimd")
 
         for i in range(-KEYS_AHEAD, UNITS):
             if 0 <= i + EXP_AHEAD < UNITS:
                 stage_exp(i + EXP_AHEAD)
+            if 0 <= i < len(SCALAR_PIECES_OF_CHUNK_1):
+                w, g = SCALAR_PIECES_OF_CHUNK_1[i]
+                regroup_weight_piece(1, w, g, "scalar")
             if i + KEYS_AHEAD < UNITS:
                 stage_keys(i + KEYS_AHEAD)
             if 0 <= i + EXP_AHEAD < UNITS:
@@ -285,7 +294,7 @@ def tile_linearattention_pa_kernel(tc, x, Wk, bk, Wv, bv, out_0, out_1):
                 continue
             c, place_in_chunk = divmod(i, UNITS_PER_CHUNK)
             more_chunks = c + 1 < CHUNKS
-            if more_chunks and place_in_chunk < len(pieces) - GPSIMD_PIECES:
+            if c >= 1 and more_chunks and place_in_chunk < len(pieces) - GPSIMD_PIECES:
                 regroup_weight_piece(c + 1, *pieces[GPSIMD_PIECES + place_in_chunk], "scalar")
             stage_sums(i)
             if more_chunks and place_in_chunk == UNITS_PER_CHUNK - KEYS_AHEAD - 1:

@@ -47,6 +47,9 @@ GPSIMD_PIECES = 3
 
 SCALAR_PIECES_OF_CHUNK_1 = ((KEY, 1), (VALUE, 1))
 
+KV, KSUM = 0, 1
+SCALAR_SUMS = ((KSUM, UNITS - 3), (KV, UNITS - 3), (KSUM, UNITS - 2))
+
 FLOPS = 2 * WEIGHTS * TOKENS * D * H
 
 
@@ -220,34 +223,56 @@ def tile_linearattention_pa_kernel(tc, x, Wk, bk, Wv, bv, out_0, out_1):
             value_acc[i] = psum.tile([P, N_MOVE], F32, tag="value_acc", name="value_acc")
             multiply(VALUE, i, value_acc[i])
 
+        k_feat = {}
+        k_value = {}
+
+        def sum_column(what, i, b):
+            c, local, half = unit_place(i)
+            column = (half * BATCHES_PER_HALF + b) * H_TILES + c * TILES_PER_CHUNK + local
+            if what == KSUM:
+                column += BATCHES * H_TILES
+            return sums[:, column : column + 1]
+
+        def vector_sum(what, i, b):
+            return None if (what, i) in SCALAR_SUMS else sum_column(what, i, b)
+
+        def scalar_sum(what, i):
+            source = k_feat[i] if what == KSUM else k_value[i]
+            for b in range(BATCHES_PER_HALF):
+                copied = work.tile([P, SEQ], F32, tag="copied")
+                nc.scalar.activation(
+                    out=copied[:],
+                    in_=source[:, b * SEQ : (b + 1) * SEQ],
+                    func=ACT.Copy,
+                    accum_out=sum_column(what, i, b),
+                )
+
         def stage_sums(i):
             c, local, half = unit_place(i)
             t = c * TILES_PER_CHUNK + local
-            k_feat = work.tile([P, N_MOVE], F32, tag="k_feat")
-            k_value = work.tile([P, N_MOVE], F32, tag="k_value")
+            k_feat[i] = work.tile([P, N_MOVE], F32, tag="k_feat", name="k_feat", bufs=4)
+            k_value[i] = work.tile([P, N_MOVE], F32, tag="k_value", name="k_value", bufs=4)
             for b in range(BATCHES_PER_HALF):
                 toks = slice(b * SEQ, (b + 1) * SEQ)
-                ksum_col = BATCHES * H_TILES + (half * BATCHES_PER_HALF + b) * H_TILES + t
                 nc.vector.scalar_tensor_tensor(
-                    out=k_feat[:, toks],
+                    out=k_feat[i][:, toks],
                     in0=key_acc[i][:, toks],
                     scalar=bk_plus_1[:, t : t + 1],
                     in1=exp_min_v_0[i][:, toks],
                     op0=ALU.add,
                     op1=ALU.max,
-                    accum_out=sums[:, ksum_col : ksum_col + 1],
+                    accum_out=vector_sum(KSUM, i, b),
                 )
             for b in range(BATCHES_PER_HALF):
                 toks = slice(b * SEQ, (b + 1) * SEQ)
-                kv_col = (half * BATCHES_PER_HALF + b) * H_TILES + t
                 nc.vector.scalar_tensor_tensor(
-                    out=k_value[:, toks],
+                    out=k_value[i][:, toks],
                     in0=value_acc[i][:, toks],
                     scalar=bv_cols[:, t : t + 1],
-                    in1=k_feat[:, toks],
+                    in1=k_feat[i][:, toks],
                     op0=ALU.add,
                     op1=ALU.mult,
-                    accum_out=sums[:, kv_col : kv_col + 1],
+                    accum_out=vector_sum(KV, i, b),
                 )
 
         transpose_x_batch(0)
@@ -271,8 +296,8 @@ def tile_linearattention_pa_kernel(tc, x, Wk, bk, Wv, bv, out_0, out_1):
         quantise_x_batch(2)
         transpose_x_batch(3)
         regroup_weight_piece(0, VALUE, 0, "vector")
-        quantise_x_batch(3)
         regroup_weight_piece(0, VALUE, 1, "vector")
+        quantise_x_batch(3)
         quantise_weight_chunk(0, VALUE)
 
         pieces = list(product(range(WEIGHTS), range(PASSES)))
@@ -297,6 +322,9 @@ def tile_linearattention_pa_kernel(tc, x, Wk, bk, Wv, bv, out_0, out_1):
             if c >= 1 and more_chunks and place_in_chunk < len(pieces) - GPSIMD_PIECES:
                 regroup_weight_piece(c + 1, *pieces[GPSIMD_PIECES + place_in_chunk], "scalar")
             stage_sums(i)
+            if i == UNITS - 1:
+                for what, unit in SCALAR_SUMS:
+                    scalar_sum(what, unit)
             if more_chunks and place_in_chunk == UNITS_PER_CHUNK - KEYS_AHEAD - 1:
                 quantise_weight_chunk(c + 1, KEY)
             if more_chunks and place_in_chunk == UNITS_PER_CHUNK - EXP_AHEAD - 1:

@@ -211,13 +211,23 @@ def tile_linearattention_pa_kernel(tc, x, Wk, bk, Wv, bv, out_0, out_1):
             key_acc[i] = psum.tile([P, N_MOVE], F32, tag="key_acc", name="key_acc")
             multiply(KEY, i, key_acc[i])
             relu_minus_v[i] = work.tile([P, N_MOVE], F32, tag="relu_minus_v", name="relu_minus_v")
-            nc.scalar.activation(
-                out=relu_minus_v[i][:], in_=key_acc[i][:], func=ACT.Relu, scale=-1.0, bias=minus_bk[:, t : t + 1]
-            )
+            for b in range(BATCHES_PER_HALF):
+                toks = slice(b * SEQ, (b + 1) * SEQ)
+                nc.scalar.activation(
+                    out=relu_minus_v[i][:, toks],
+                    in_=key_acc[i][:, toks],
+                    func=ACT.Relu,
+                    scale=-1.0,
+                    bias=minus_bk[:, t : t + 1],
+                )
 
         def stage_exp(i):
             exp_min_v_0[i] = work.tile([P, N_MOVE], F32, tag="exp_min_v_0", name="exp_min_v_0")
-            nc.scalar.activation(out=exp_min_v_0[i][:], in_=relu_minus_v[i][:], func=ACT.Exp, scale=-1.0)
+            for b in range(BATCHES_PER_HALF):
+                toks = slice(b * SEQ, (b + 1) * SEQ)
+                nc.scalar.activation(
+                    out=exp_min_v_0[i][:, toks], in_=relu_minus_v[i][:, toks], func=ACT.Exp, scale=-1.0
+                )
 
         def stage_values(i):
             value_acc[i] = psum.tile([P, N_MOVE], F32, tag="value_acc", name="value_acc")

@@ -43,9 +43,7 @@ RUN = 8
 KEYS_AHEAD = 2
 EXP_AHEAD = 1
 
-GPSIMD_PIECES = 3
-
-SCALAR_PIECES_OF_CHUNK_1 = ((KEY, 1), (VALUE, 1))
+SCALAR_PIECES = ((KEY, 1), (VALUE, 1))
 
 KV, KSUM = 0, 1
 SCALAR_SUMS = ((KSUM, UNITS - 3), (KV, UNITS - 3), (KSUM, UNITS - 2))
@@ -310,27 +308,26 @@ def tile_linearattention_pa_kernel(tc, x, Wk, bk, Wv, bv, out_0, out_1):
         quantise_x_batch(3)
         quantise_weight_chunk(0, VALUE)
 
-        pieces = list(product(range(WEIGHTS), range(PASSES)))
-        for w, g in pieces:
-            if (w, g) not in SCALAR_PIECES_OF_CHUNK_1:
-                regroup_weight_piece(1, w, g, "gpsimd")
+        def regroup_on_gpsimd(c):
+            for w, g in product(range(WEIGHTS), range(PASSES)):
+                if (w, g) not in SCALAR_PIECES:
+                    regroup_weight_piece(c, w, g, "gpsimd")
+
+        regroup_on_gpsimd(1)
 
         for i in range(-KEYS_AHEAD, UNITS):
             if 0 <= i + EXP_AHEAD < UNITS:
                 stage_exp(i + EXP_AHEAD)
-            if 0 <= i < len(SCALAR_PIECES_OF_CHUNK_1):
-                w, g = SCALAR_PIECES_OF_CHUNK_1[i]
-                regroup_weight_piece(1, w, g, "scalar")
+            c, place_in_chunk = divmod(i, UNITS_PER_CHUNK)
+            more_chunks = c + 1 < CHUNKS
+            if i >= 0 and more_chunks and place_in_chunk < len(SCALAR_PIECES):
+                regroup_weight_piece(c + 1, *SCALAR_PIECES[place_in_chunk], "scalar")
             if i + KEYS_AHEAD < UNITS:
                 stage_keys(i + KEYS_AHEAD)
             if 0 <= i + EXP_AHEAD < UNITS:
                 stage_values(i + EXP_AHEAD)
             if i < 0:
                 continue
-            c, place_in_chunk = divmod(i, UNITS_PER_CHUNK)
-            more_chunks = c + 1 < CHUNKS
-            if c >= 1 and more_chunks and place_in_chunk < len(pieces) - GPSIMD_PIECES:
-                regroup_weight_piece(c + 1, *pieces[GPSIMD_PIECES + place_in_chunk], "scalar")
             stage_sums(i)
             if i == UNITS - 1:
                 for what, unit in SCALAR_SUMS:
@@ -340,8 +337,7 @@ def tile_linearattention_pa_kernel(tc, x, Wk, bk, Wv, bv, out_0, out_1):
             if more_chunks and place_in_chunk == UNITS_PER_CHUNK - EXP_AHEAD - 1:
                 quantise_weight_chunk(c + 1, VALUE)
                 if c + 2 < CHUNKS:
-                    for w, g in pieces[:GPSIMD_PIECES]:
-                        regroup_weight_piece(c + 2, w, g, "gpsimd")
+                    regroup_on_gpsimd(c + 2)
 
         sums_ps = psum.tile([P, P], F32, tag="key_acc")
         nc.tensor.transpose(out=sums_ps[:], in_=sums[:], identity=ident[:])

@@ -32,7 +32,7 @@ CHUNK = 256
 CHUNKS = H // CHUNK
 TILES_PER_CHUNK = CHUNK // P
 WEIGHTS = 2
-PIECES = WEIGHTS * PASSES * CHUNKS
+LOADS_OF_A_SIZE = WEIGHTS * PASSES * (CHUNKS // 2)
 KEY, VALUE = 0, 1
 
 UNITS = H_TILES * HALVES
@@ -60,7 +60,7 @@ def tile_linearattention_pa_kernel(tc, x, Wk, bk, Wv, bv, out_0, out_1):
         ctx.enter_context(tc.manual_schedule())
         consts = ctx.enter_context(tc.tile_pool(name="consts", bufs=1))
         x_pool = ctx.enter_context(tc.tile_pool(name="x_pool", bufs=1))
-        w_pool = ctx.enter_context(tc.tile_pool(name="w_pool", bufs=PIECES))
+        w_pool = ctx.enter_context(tc.tile_pool(name="w_pool", bufs=LOADS_OF_A_SIZE))
         group_pool = ctx.enter_context(tc.tile_pool(name="group_pool", bufs=1))
         work = ctx.enter_context(tc.tile_pool(name="work", bufs=3))
         psum = ctx.enter_context(tc.psum_pool(name="psum", bufs=4))
@@ -81,23 +81,23 @@ def tile_linearattention_pa_kernel(tc, x, Wk, bk, Wv, bv, out_0, out_1):
                 nc.sync.dma_start(out=raw[:], in_=x_rows[first : first + P, :])
                 x_raw[(b, a)] = raw
 
-        def load_weight_chunk(c, w):
+        def load_weight_chunks(first, count, w):
             for g in range(PASSES):
-                raw = w_pool.tile([P, PACK, CHUNK], BF16, tag="w_raw")
+                raw = w_pool.tile([P, PACK, count * CHUNK], BF16, tag="w_raw" + str(count))
+                columns = slice(first * CHUNK, (first + count) * CHUNK)
                 nc.sync.dma_start(
                     out=raw[:],
-                    in_=weights[w][g * K_PASS : (g + 1) * K_PASS, c * CHUNK : (c + 1) * CHUNK].rearrange(
-                        "(p j) c -> p j c", j=PACK
-                    ),
+                    in_=weights[w][g * K_PASS : (g + 1) * K_PASS, columns].rearrange("(p j) c -> p j c", j=PACK),
                 )
-                w_raw[(c, w, g)] = raw
+                for member in range(count):
+                    w_raw[(first + member, w, g)] = raw[:, :, member * CHUNK : (member + 1) * CHUNK]
 
         load_x_batches(0, 1)
-        load_weight_chunk(0, KEY)
+        load_weight_chunks(0, 1, KEY)
         load_x_batches(2, 3)
-        load_weight_chunk(0, VALUE)
-        for c, w in product(range(1, CHUNKS), range(WEIGHTS)):
-            load_weight_chunk(c, w)
+        load_weight_chunks(0, 1, VALUE)
+        for (first, count), w in product(((1, 1), (2, 2)), range(WEIGHTS)):
+            load_weight_chunks(first, count, w)
 
         ident = consts.tile([P, P], F32)
         make_identity(nc, ident[:])
@@ -150,7 +150,7 @@ def tile_linearattention_pa_kernel(tc, x, Wk, bk, Wv, bv, out_0, out_1):
                     [P, WEIGHTS, PASSES, CHUNK, PACK], BF16, align_bytes=64, name="w_grouped", tag="w_grouped"
                 )
             grouped = w_grouped[c][:, w, g]
-            raw = w_raw[(c, w, g)][:]
+            raw = w_raw[(c, w, g)]
             if engine == "gpsimd":
                 nc.gpsimd.tensor_scalar(
                     out=grouped,

@@ -46,7 +46,12 @@ EXP_AHEAD = 1
 SCALAR_PIECES = ((KEY, 1), (VALUE, 1))
 
 KV, KSUM = 0, 1
-SCALAR_SUMS = ((KSUM, UNITS - 3), (KV, UNITS - 3), (KSUM, UNITS - 2))
+BLOCK = 32
+SCALAR_SUMS = ((KSUM, UNITS - 3), (KV, UNITS - 3))
+
+FOLDED_PAIRS = {UNITS - 8: (UNITS - 6, UNITS - 2), UNITS - 6: (UNITS - 4, UNITS - 1)}
+FOLDED_UNITS = [first + member for first in FOLDED_PAIRS for member in range(TILES_PER_CHUNK)]
+FOLDS = 4
 
 FLOPS = 2 * WEIGHTS * TOKENS * D * H
 
@@ -106,8 +111,7 @@ def tile_linearattention_pa_kernel(tc, x, Wk, bk, Wv, bv, out_0, out_1):
         nc.vector.memset(warm[:], 0.0)
         nc.scalar.activation(out=warm[:], in_=warm[:], func=ACT.Exp)
 
-        sums = consts.tile([P, P], F32)
-        nc.vector.memset(sums[:], 0.0)
+        sums = consts.tile([P, 2 * BLOCK], F32, align_bytes=64)
 
         x_grouped = {}
         x_quant = {}
@@ -242,7 +246,33 @@ def tile_linearattention_pa_kernel(tc, x, Wk, bk, Wv, bv, out_0, out_1):
             return sums[:, column : column + 1]
 
         def vector_sum(what, i, b):
-            return None if (what, i) in SCALAR_SUMS else sum_column(what, i, b)
+            elsewhere = (what, i) in SCALAR_SUMS or (what == KV and i in FOLDED_UNITS)
+            return None if elsewhere else sum_column(what, i, b)
+
+        pair_value = {}
+        folded = {}
+
+        def fold_pair(first):
+            rest = pair_value[first][:].rearrange("p l (b k) -> p (l b) k", k=SEQ)
+            n = SEQ
+            for step in range(FOLDS):
+                n //= 2
+                part = work.tile([P, TILES_PER_CHUNK * BATCHES_PER_HALF, n], F32, tag="part" + str(n), name="part", bufs=2)
+                nc.gpsimd.tensor_tensor(out=part[:], in0=rest[:, :, 0:n], in1=rest[:, :, n : 2 * n], op=ALU.add)
+                rest = part[:]
+            folded[first] = rest
+
+        def sum_folded_pair(first):
+            c, local, half = unit_place(first)
+            t = c * TILES_PER_CHUNK
+            b = half * BATCHES_PER_HALF
+            columns = sums[:, 0 : BATCHES * H_TILES].rearrange("p (n t) -> p t n", t=H_TILES)
+            nc.vector.tensor_reduce(
+                out=columns[:, t : t + TILES_PER_CHUNK, b : b + BATCHES_PER_HALF],
+                in_=folded[first].rearrange("p (l b) k -> p l b k", b=BATCHES_PER_HALF),
+                op=ALU.add,
+                axis=mybir.AxisListType.X,
+            )
 
         def scalar_sum(what, i):
             source = k_feat[i] if what == KSUM else k_value[i]
@@ -259,7 +289,14 @@ def tile_linearattention_pa_kernel(tc, x, Wk, bk, Wv, bv, out_0, out_1):
             c, local, half = unit_place(i)
             t = c * TILES_PER_CHUNK + local
             k_feat[i] = work.tile([P, N_MOVE], F32, tag="k_feat", name="k_feat", bufs=4)
-            k_value[i] = work.tile([P, N_MOVE], F32, tag="k_value", name="k_value", bufs=4)
+            if i in FOLDED_UNITS:
+                if i in FOLDED_PAIRS:
+                    pair_value[i] = work.tile(
+                        [P, TILES_PER_CHUNK, N_MOVE], F32, tag="pair_value", name="pair_value", bufs=2
+                    )
+                k_value[i] = pair_value[i - local][:, local]
+            else:
+                k_value[i] = work.tile([P, N_MOVE], F32, tag="k_value", name="k_value", bufs=4)
             for b in range(BATCHES_PER_HALF):
                 toks = slice(b * SEQ, (b + 1) * SEQ)
                 nc.vector.scalar_tensor_tensor(
@@ -329,6 +366,12 @@ def tile_linearattention_pa_kernel(tc, x, Wk, bk, Wv, bv, out_0, out_1):
             if i < 0:
                 continue
             stage_sums(i)
+            for first in FOLDED_PAIRS:
+                fold_turn, sum_turn = FOLDED_PAIRS[first]
+                if i == fold_turn:
+                    fold_pair(first)
+                if i == sum_turn:
+                    sum_folded_pair(first)
             if i == UNITS - 1:
                 for what, unit in SCALAR_SUMS:
                     scalar_sum(what, unit)
@@ -339,10 +382,11 @@ def tile_linearattention_pa_kernel(tc, x, Wk, bk, Wv, bv, out_0, out_1):
                 if c + 2 < CHUNKS:
                     regroup_on_gpsimd(c + 2)
 
-        sums_ps = psum.tile([P, P], F32, tag="key_acc")
-        nc.tensor.transpose(out=sums_ps[:], in_=sums[:], identity=ident[:])
-        result = consts.tile([P, P], F32)
-        nc.vector.tensor_copy(out=result[:], in_=sums_ps[:])
-        rows = BATCHES * H_TILES
-        nc.sync.dma_start(out=out_0.rearrange("n (t p) -> (n t) p", p=P), in_=result[0:rows, :])
-        nc.sync.dma_start(out=out_1.rearrange("n (t p) -> (n t) p", p=P), in_=result[rows : 2 * rows, :])
+        result = consts.tile([P, 2, BLOCK], F32, align_bytes=64)
+        for what, out in enumerate((out_0, out_1)):
+            nc.vector.transpose(out=result[:, what, :], in_=sums[:, what * BLOCK : (what + 1) * BLOCK])
+        for what, out in enumerate((out_0, out_1)):
+            rows = out.rearrange("n (t a j) -> a (n t) j", a=P // BLOCK, j=BLOCK)
+            queue = (nc.sync, nc.scalar)[what]
+            for a in range(P // BLOCK):
+                queue.dma_start(out=rows[a], in_=result[a * BLOCK : (a + 1) * BLOCK, what, :])

from contextlib import ExitStack
from itertools import product

import concourse.mybir as mybir
from concourse.masks import make_identity

F32 = mybir.dt.float32
BF16 = mybir.dt.bfloat16
U32 = mybir.dt.uint32
U8 = mybir.dt.uint8
FP8X4 = mybir.dt.float8_e4m3fn_x4
ALU = mybir.AluOpType
ACT = mybir.ActivationFunctionType

BATCHES, SEQ, D, H = 4, 256, 1024, 1024
TOKENS = BATCHES * SEQ

P = 128
PACK = 4
K_PASS = P * PACK
PASSES = D // K_PASS
WORDS = PACK // 2

N_MOVE = 512
HALVES = TOKENS // N_MOVE
TOKEN_TILES = TOKENS // P
TILES_PER_BATCH = SEQ // P
BATCHES_PER_HALF = N_MOVE // SEQ

H_TILES = H // P
CHUNK = 256
CHUNKS = H // CHUNK
TILES_PER_CHUNK = CHUNK // P
WEIGHTS = 2
LOADS_OF_A_SIZE = WEIGHTS * PASSES * (CHUNKS // 2)
KEY, VALUE = 0, 1

UNITS = H_TILES * HALVES
UNITS_PER_CHUNK = TILES_PER_CHUNK * HALVES

RUN = 8

KEYS_AHEAD = 2
EXP_AHEAD = 1

SCALAR_PIECES = ((KEY, 1), (VALUE, 1))

KV, KSUM = 0, 1
BLOCK = 32
SCALAR_SUMS = ((KSUM, UNITS - 3), (KV, UNITS - 3))

FOLDED_PAIRS = {UNITS - 8: (UNITS - 6, UNITS - 2), UNITS - 6: (UNITS - 4, UNITS - 1)}
FOLDED_UNITS = [first + member for first in FOLDED_PAIRS for member in range(TILES_PER_CHUNK)]
FOLDS = 4

FLOPS = 2 * WEIGHTS * TOKENS * D * H


def tile_linearattention_pa_kernel(tc, x, Wk, bk, Wv, bv, out_0, out_1):
    nc = tc.nc
    x_rows = x.rearrange("n s d -> (n s) d")
    weights = (Wk, Wv)

    with ExitStack() as ctx:
        ctx.enter_context(tc.manual_schedule())
        consts = ctx.enter_context(tc.tile_pool(name="consts", bufs=1))
        x_pool = ctx.enter_context(tc.tile_pool(name="x_pool", bufs=1))
        w_pool = ctx.enter_context(tc.tile_pool(name="w_pool", bufs=LOADS_OF_A_SIZE))
        group_pool = ctx.enter_context(tc.tile_pool(name="group_pool", bufs=1))
        work = ctx.enter_context(tc.tile_pool(name="work", bufs=3))
        psum = ctx.enter_context(tc.psum_pool(name="psum", bufs=4))
        bank_tags = ("key_acc", "value_acc")

        bias_rows = consts.tile([P, P], BF16)
        nc.vector.memset(bias_rows[:], 0.0)
        nc.scalar.dma_start(out=bias_rows[0:H_TILES, :], in_=bk.rearrange("(t p) -> t p", p=P))
        nc.scalar.dma_start(out=bias_rows[H_TILES : 2 * H_TILES, :], in_=bv.rearrange("(t p) -> t p", p=P))

        x_raw = {}
        w_raw = {}

        def load_x_batches(*batches):
            for b, a in product(batches, range(TILES_PER_BATCH)):
                raw = x_pool.tile([P, D], BF16, tag="x_raw", bufs=TOKEN_TILES)
                first = b * SEQ + a * P
                nc.sync.dma_start(out=raw[:], in_=x_rows[first : first + P, :])
                x_raw[(b, a)] = raw

        def load_weight_chunks(first, count, w):
            for g in range(PASSES):
                raw = w_pool.tile([P, PACK, count * CHUNK], BF16, tag="w_raw" + str(count))
                columns = slice(first * CHUNK, (first + count) * CHUNK)
                nc.sync.dma_start(
                    out=raw[:],
                    in_=weights[w][g * K_PASS : (g + 1) * K_PASS, columns].rearrange("(p j) c -> p j c", j=PACK),
                )
                for member in range(count):
                    w_raw[(first + member, w, g)] = raw[:, :, member * CHUNK : (member + 1) * CHUNK]

        load_x_batches(0, 1)
        load_weight_chunks(0, 1, KEY)
        load_x_batches(2, 3)
        load_weight_chunks(0, 1, VALUE)
        for (first, count), w in product(((1, 1), (2, 2)), range(WEIGHTS)):
            load_weight_chunks(first, count, w)

        ident = consts.tile([P, P], F32)
        make_identity(nc, ident[:])

        warm = consts.tile([P, 1], F32)
        nc.vector.memset(warm[:], 0.0)
        nc.scalar.activation(out=warm[:], in_=warm[:], func=ACT.Exp)

        sums = consts.tile([P, 2 * BLOCK], F32, align_bytes=64)

        x_grouped = {}
        x_quant = {}

        def transpose_x_batch(b):
            grouped = x_pool.tile([P, PASSES * SEQ * PACK], BF16, align_bytes=64, tag="x_grouped", bufs=BATCHES)
            grouped_words = grouped[:].bitcast(F32).rearrange("p (g t u) -> p g t u", g=PASSES, u=WORDS)
            for a in range(TILES_PER_BATCH):
                words = x_raw[(b, a)][:].bitcast(F32).rearrange("p (g q u) -> p g u q", g=PASSES, u=WORDS)
                transposed = psum.tile([P, PASSES, WORDS, P], F32, tag=bank_tags[a % 2])
                for g, u in product(range(PASSES), range(WORDS)):
                    nc.tensor.transpose(out=transposed[:, g, u, :], in_=words[:, g, u, :], identity=ident[:])
                nc.scalar.copy(
                    out=grouped_words[:, :, a * P : (a + 1) * P, :],
                    in_=transposed[:].rearrange("p g u t -> p g t u"),
                )
            x_grouped[b] = grouped

        def quantise_x_batch(b):
            half, place = divmod(b, BATCHES_PER_HALF)
            toks = slice(place * SEQ, (place + 1) * SEQ)
            for g in range(PASSES):
                if place == 0:
                    codes = x_pool.tile([P, N_MOVE], U32, align_bytes=64, tag="x_codes", bufs=HALVES * PASSES)
                    scales = x_pool.tile([P, N_MOVE], U8, align_bytes=64, tag="x_scales", bufs=HALVES * PASSES)
                    x_quant[(g, half)] = (codes, scales)
                codes, scales = x_quant[(g, half)]
                nc.vector.quantize_mx(
                    out=codes[:, toks].bitcast(FP8X4),
                    scales=scales[:, toks],
                    in_=x_grouped[b][:, g * SEQ * PACK : (g + 1) * SEQ * PACK],
                )

        w_grouped = {}
        w_quant = {}

        def regroup_weight_piece(c, w, g, engine):
            if c not in w_grouped:
                w_grouped[c] = group_pool.tile(
                    [P, WEIGHTS, PASSES, CHUNK, PACK], BF16, align_bytes=64, name="w_grouped", tag="w_grouped"
                )
            grouped = w_grouped[c][:, w, g]
            raw = w_raw[(c, w, g)]
            if engine == "gpsimd":
                nc.gpsimd.tensor_scalar(
                    out=grouped,
                    in0=raw.rearrange("p j c -> p c j"),
                    scalar1=1.0,
                    scalar2=0.0,
                    op0=ALU.mult,
                    op1=ALU.add,
                )
            else:
                copy = nc.vector.tensor_copy if engine == "vector" else nc.scalar.copy
                copy(
                    out=grouped.rearrange("p (c i) j -> p c j i", i=RUN),
                    in_=raw.rearrange("p j (c i) -> p c j i", i=RUN),
                )

        def quantise_weight_chunk(c, w):
            codes = w_pool.tile([P, PASSES, CHUNK], U32, align_bytes=64, tag="w_codes", bufs=WEIGHTS * CHUNKS)
            scales = w_pool.tile([P, PASSES, CHUNK], U8, align_bytes=64, tag="w_scales", bufs=WEIGHTS * CHUNKS)
            nc.vector.quantize_mx(
                out=codes[:].rearrange("p g c -> p (g c)").bitcast(FP8X4),
                scales=scales[:].rearrange("p g c -> p (g c)"),
                in_=w_grouped[c][:, w].rearrange("p g c j -> p (g c j)"),
            )
            w_quant[(c, w)] = (codes, scales)

        def unit_place(i):
            c, rest = divmod(i, UNITS_PER_CHUNK)
            half, local = divmod(rest, TILES_PER_CHUNK)
            return c, local, half

        def multiply(w, i, acc):
            c, local, half = unit_place(i)
            cols = slice(local * P, (local + 1) * P)
            w_codes, w_scales = w_quant[(c, w)]
            for g in range(PASSES):
                x_codes, x_scales = x_quant[(g, half)]
                nc.tensor.matmul_mx(
                    out=acc[:],
                    lhsT=w_codes[:, g, cols].bitcast(FP8X4),
                    lhsT_scale=w_scales[:, g, cols],
                    rhs=x_codes[:].bitcast(FP8X4),
                    rhs_scale=x_scales[:],
                    start=(g == 0),
                    stop=(g == PASSES - 1),
                )

        key_acc = {}
        value_acc = {}
        relu_minus_v = {}
        exp_min_v_0 = {}

        def stage_keys(i):
            c, local, half = unit_place(i)
            t = c * TILES_PER_CHUNK + local
            key_acc[i] = psum.tile([P, N_MOVE], F32, tag="key_acc", name="key_acc")
            multiply(KEY, i, key_acc[i])
            relu_minus_v[i] = work.tile([P, N_MOVE], F32, tag="relu_minus_v", name="relu_minus_v")
            for b in range(BATCHES_PER_HALF):
                toks = slice(b * SEQ, (b + 1) * SEQ)
                nc.scalar.activation(
                    out=relu_minus_v[i][:, toks],
                    in_=key_acc[i][:, toks],
                    func=ACT.Relu,
                    scale=-1.0,
                    bias=minus_bk[:, t : t + 1],
                )

        def stage_exp(i):
            exp_min_v_0[i] = work.tile([P, N_MOVE], F32, tag="exp_min_v_0", name="exp_min_v_0")
            for b in range(BATCHES_PER_HALF):
                toks = slice(b * SEQ, (b + 1) * SEQ)
                nc.scalar.activation(
                    out=exp_min_v_0[i][:, toks], in_=relu_minus_v[i][:, toks], func=ACT.Exp, scale=-1.0
                )

        def stage_values(i):
            value_acc[i] = psum.tile([P, N_MOVE], F32, tag="value_acc", name="value_acc")
            multiply(VALUE, i, value_acc[i])

        k_feat = {}
        k_value = {}

        def sum_column(what, i, b):
            c, local, half = unit_place(i)
            column = (half * BATCHES_PER_HALF + b) * H_TILES + c * TILES_PER_CHUNK + local
            if what == KSUM:
                column += BATCHES * H_TILES
            return sums[:, column : column + 1]

        def vector_sum(what, i, b):
            elsewhere = (what, i) in SCALAR_SUMS or (what == KV and i in FOLDED_UNITS)
            return None if elsewhere else sum_column(what, i, b)

        pair_value = {}
        folded = {}

        def fold_pair(first):
            rest = pair_value[first][:].rearrange("p l (b k) -> p (l b) k", k=SEQ)
            n = SEQ
            for step in range(FOLDS):
                n //= 2
                part = work.tile([P, TILES_PER_CHUNK * BATCHES_PER_HALF, n], F32, tag="part" + str(n), name="part", bufs=2)
                nc.gpsimd.tensor_tensor(out=part[:], in0=rest[:, :, 0:n], in1=rest[:, :, n : 2 * n], op=ALU.add)
                rest = part[:]
            folded[first] = rest

        def sum_folded_pair(first):
            c, local, half = unit_place(first)
            t = c * TILES_PER_CHUNK
            b = half * BATCHES_PER_HALF
            columns = sums[:, 0 : BATCHES * H_TILES].rearrange("p (n t) -> p t n", t=H_TILES)
            nc.vector.tensor_reduce(
                out=columns[:, t : t + TILES_PER_CHUNK, b : b + BATCHES_PER_HALF],
                in_=folded[first].rearrange("p (l b) k -> p l b k", b=BATCHES_PER_HALF),
                op=ALU.add,
                axis=mybir.AxisListType.X,
            )

        def scalar_sum(what, i):
            source = k_feat[i] if what == KSUM else k_value[i]
            for b in range(BATCHES_PER_HALF):
                copied = work.tile([P, SEQ], F32, tag="copied")
                nc.scalar.activation(
                    out=copied[:],
                    in_=source[:, b * SEQ : (b + 1) * SEQ],
                    func=ACT.Copy,
                    accum_out=sum_column(what, i, b),
                )

        def stage_sums(i):
            c, local, half = unit_place(i)
            t = c * TILES_PER_CHUNK + local
            k_feat[i] = work.tile([P, N_MOVE], F32, tag="k_feat", name="k_feat", bufs=4)
            if i in FOLDED_UNITS:
                if i in FOLDED_PAIRS:
                    pair_value[i] = work.tile(
                        [P, TILES_PER_CHUNK, N_MOVE], F32, tag="pair_value", name="pair_value", bufs=2
                    )
                k_value[i] = pair_value[i - local][:, local]
            else:
                k_value[i] = work.tile([P, N_MOVE], F32, tag="k_value", name="k_value", bufs=4)
            for b in range(BATCHES_PER_HALF):
                toks = slice(b * SEQ, (b + 1) * SEQ)
                nc.vector.scalar_tensor_tensor(
                    out=k_feat[i][:, toks],
                    in0=key_acc[i][:, toks],
                    scalar=bk_plus_1[:, t : t + 1],
                    in1=exp_min_v_0[i][:, toks],
                    op0=ALU.add,
                    op1=ALU.max,
                    accum_out=vector_sum(KSUM, i, b),
                )
            for b in range(BATCHES_PER_HALF):
                toks = slice(b * SEQ, (b + 1) * SEQ)
                nc.vector.scalar_tensor_tensor(
                    out=k_value[i][:, toks],
                    in0=value_acc[i][:, toks],
                    scalar=bv_cols[:, t : t + 1],
                    in1=k_feat[i][:, toks],
                    op0=ALU.add,
                    op1=ALU.mult,
                    accum_out=vector_sum(KV, i, b),
                )

        transpose_x_batch(0)
        quantise_x_batch(0)
        transpose_x_batch(1)
        regroup_weight_piece(0, KEY, 0, "vector")
        bias_rows_f32 = consts.tile([P, P], F32)
        nc.vector.tensor_copy(out=bias_rows_f32[:], in_=bias_rows[:])
        bias_ps = psum.tile([P, P], F32, tag="key_acc")
        nc.tensor.transpose(out=bias_ps[:], in_=bias_rows_f32[:], identity=ident[:])
        quantise_x_batch(1)
        regroup_weight_piece(0, KEY, 1, "vector")
        quantise_weight_chunk(0, KEY)
        bv_cols = consts.tile([P, H_TILES], F32)
        nc.vector.tensor_copy(out=bv_cols[:], in_=bias_ps[:, H_TILES : 2 * H_TILES])
        bk_plus_1 = consts.tile([P, H_TILES], F32)
        nc.vector.tensor_scalar_add(out=bk_plus_1[:], in0=bias_ps[:, 0:H_TILES], scalar1=1.0)
        minus_bk = consts.tile([P, H_TILES], F32)
        nc.vector.tensor_scalar_mul(out=minus_bk[:], in0=bias_ps[:, 0:H_TILES], scalar1=-1.0)
        transpose_x_batch(2)
        quantise_x_batch(2)
        transpose_x_batch(3)
        regroup_weight_piece(0, VALUE, 0, "vector")
        regroup_weight_piece(0, VALUE, 1, "vector")
        quantise_x_batch(3)
        quantise_weight_chunk(0, VALUE)

        def regroup_on_gpsimd(c):
            for w, g in product(range(WEIGHTS), range(PASSES)):
                if (w, g) not in SCALAR_PIECES:
                    regroup_weight_piece(c, w, g, "gpsimd")

        regroup_on_gpsimd(1)

        for i in range(-KEYS_AHEAD, UNITS):
            if 0 <= i + EXP_AHEAD < UNITS:
                stage_exp(i + EXP_AHEAD)
            c, place_in_chunk = divmod(i, UNITS_PER_CHUNK)
            more_chunks = c + 1 < CHUNKS
            if i >= 0 and more_chunks and place_in_chunk < len(SCALAR_PIECES):
                regroup_weight_piece(c + 1, *SCALAR_PIECES[place_in_chunk], "scalar")
            if i + KEYS_AHEAD < UNITS:
                stage_keys(i + KEYS_AHEAD)
            if 0 <= i + EXP_AHEAD < UNITS:
                stage_values(i + EXP_AHEAD)
            if i < 0:
                continue
            stage_sums(i)
            for first in FOLDED_PAIRS:
                fold_turn, sum_turn = FOLDED_PAIRS[first]
                if i == fold_turn:
                    fold_pair(first)
                if i == sum_turn:
                    sum_folded_pair(first)
            if i == UNITS - 1:
                for what, unit in SCALAR_SUMS:
                    scalar_sum(what, unit)
            if more_chunks and place_in_chunk == UNITS_PER_CHUNK - KEYS_AHEAD - 1:
                quantise_weight_chunk(c + 1, KEY)
            if more_chunks and place_in_chunk == UNITS_PER_CHUNK - EXP_AHEAD - 1:
                quantise_weight_chunk(c + 1, VALUE)
                if c + 2 < CHUNKS:
                    regroup_on_gpsimd(c + 2)

        result = consts.tile([P, 2, BLOCK], F32, align_bytes=64)
        for what, out in enumerate((out_0, out_1)):
            nc.vector.transpose(out=result[:, what, :], in_=sums[:, what * BLOCK : (what + 1) * BLOCK])
        for what, out in enumerate((out_0, out_1)):
            rows = out.rearrange("n (t a j) -> a (n t) j", a=P // BLOCK, j=BLOCK)
            queue = (nc.sync, nc.scalar)[what]
            for a in range(P // BLOCK):
                queue.dma_start(out=rows[a], in_=result[a * BLOCK : (a + 1) * BLOCK, what, :])
